import numpy as np
import ml_dtypes


def mxq(x, axis, fmt="e4m3"):
    dtype, down = {"e4m3": (ml_dtypes.float8_e4m3fn, 7), "e5m2": (ml_dtypes.float8_e5m2, 14)}[fmt]
    v = np.moveaxis(np.asarray(x, np.float32).astype(ml_dtypes.bfloat16).astype(np.float64), axis, -1)
    blocks = v.reshape(v.shape[:-1] + (-1, 32))
    amax = np.abs(blocks).max(-1, keepdims=True)
    byte = np.maximum(np.where(amax > 0, np.frexp(amax)[1] - 1 + 127, 0) - down, 1)
    scale = np.exp2(byte - 127.0)
    codes = (blocks / scale).astype(np.float32).astype(dtype).astype(np.float64)
    return np.moveaxis((codes * scale).reshape(v.shape), -1, axis)


WIDE = False


def mx_kscale(k):
    if not WIDE:
        return np.ones(k)
    levels = np.array([10, -10, 5, -5, 0])
    a = np.random.permutation(np.resize(levels, k // 512 * 4)).reshape(k // 512, 4)
    idx = np.arange(k)
    return np.exp2(a[idx // 512, idx % 128 // 32])


BF16 = ml_dtypes.bfloat16


def bf(x):
    return np.asarray(x, np.float32).astype(BF16)


def f64(x):
    return np.asarray(x).astype(np.float64)


B, L, D, NH, F = 2, 2048, 512, 8, 4096
HD = D // NH
EPS = 1e-6
QUIET = 2e-3


def rmsnorm(x, w):
    return w * x * (1.0 / np.sqrt(np.mean(x * x, axis=-1, keepdims=True) + EPS))


def heads(y):
    return y.reshape(B, L, NH, HD).transpose(0, 2, 1, 3)


def setup_inputs():
    s = mx_kscale(D)
    amp = np.where(np.random.random((B, L, 1)) < 0.25, QUIET, 1.0)
    return {"x": bf(np.random.standard_normal((B, L, D)) * amp),
            "attn_norm_w": bf((1.0 + 0.1 * np.random.standard_normal(D)) * s),
            "W_q": bf(np.random.standard_normal((D, D)) / np.sqrt(D) / s),
            "W_k": bf(np.random.standard_normal((D, D)) / np.sqrt(D) / s),
            "W_v": bf(np.random.standard_normal((D, D)) * 2.0 / np.sqrt(D) / s)}


def reference(x, attn_norm_w, W_q, W_k, W_v):
    xq = mxq(rmsnorm(f64(x), f64(attn_norm_w)), 2, "e4m3")
    q = xq @ mxq(f64(W_q), 1, "e4m3").T
    k = xq @ mxq(f64(W_k), 1, "e4m3").T
    v = xq @ mxq(f64(W_v), 1, "e4m3").T
    return heads(q), heads(k), heads(v)

@@ -1,0 +1,244 @@
+from contextlib import ExitStack
+
+import concourse.mybir as mybir
+from concourse.masks import make_identity
+
+BF16 = mybir.dt.bfloat16
+F32 = mybir.dt.float32
+U32 = mybir.dt.uint32
+U8 = mybir.dt.uint8
+FP8X4 = mybir.dt.float8_e4m3fn_x4
+MULT = mybir.AluOpType.mult
+FUNC = mybir.ActivationFunctionType
+
+P = 128
+PACK = 4
+D = P * PACK
+BATCH = 2
+SEQ = 2048
+HEADS = 8
+HEAD_DIM = D // HEADS
+EPS = 1e-6
+PROJECTIONS = 3
+
+CHUNK_TILES = 8
+CHUNK_TOKENS = P * CHUNK_TILES
+CHUNKS_PER_BATCH = SEQ // CHUNK_TOKENS
+CHUNKS = BATCH * CHUNKS_PER_BATCH
+TOKEN_TILES = CHUNKS * CHUNK_TILES
+LOAD_TILES = 4
+
+PAIR = 2
+PAIRS = TOKEN_TILES // PAIR
+STEP_BANKS = PAIR * PROJECTIONS
+STEPS = PAIRS
+QUANT_LEAD = 3
+STATS_LEAD = 5
+
+FLOPS = 2 * BATCH * SEQ * D * PROJECTIONS * D
+
+
+def tile_block_pa_t_kernel(tc, x, attn_norm_w, W_q, W_k, W_v, out_0, out_1, out_2):
+    nc = tc.nc
+    weights = (W_q, W_k, W_v)
+    outs = (out_0, out_1, out_2)
+    x_chunks = x.flatten_outer_dims().rearrange("(c p g) d -> c p g d", p=P, g=CHUNK_TILES)
+
+    with ExitStack() as stack:
+        keep = stack.enter_context(tc.tile_pool(name="keep", bufs=1))
+        junk_pool = stack.enter_context(tc.tile_pool(name="junk", bufs=2))
+        scaled_pool = stack.enter_context(tc.tile_pool(name="scaled", bufs=3))
+        normed_pool = stack.enter_context(tc.tile_pool(name="normed", bufs=2))
+        w_grouped_pool = stack.enter_context(tc.tile_pool(name="w_grouped", bufs=2))
+        unit_pool = stack.enter_context(tc.tile_pool(name="unit", bufs=6))
+        flip_pool = stack.enter_context(tc.psum_pool(name="flip", bufs=2))
+        acc_pool = stack.enter_context(tc.psum_pool(name="acc", bufs=STEP_BANKS))
+
+        x_sb = keep.tile([P, TOKEN_TILES, D], BF16)
+        w_sb = keep.tile([P, PROJECTIONS, PACK, D], BF16)
+        w_codes = keep.tile([P, PROJECTIONS, D], U32, align_bytes=64)
+        w_scales = keep.tile([P, PROJECTIONS, D], U8, align_bytes=64)
+        x_codes = keep.tile([P, TOKEN_TILES * P], U32, align_bytes=64)
+        x_scales = keep.tile([P, TOKEN_TILES * P], U8, align_bytes=64)
+        sum_sq = keep.tile([P, TOKEN_TILES], F32)
+        rms = keep.tile([P, TOKEN_TILES], F32)
+        inv_rms = keep.tile([P, TOKEN_TILES], F32)
+        ident_f32 = keep.tile([P, P], F32)
+        eps_col = keep.tile([P, 1], F32)
+        table_warm = keep.tile([P, 1], F32)
+        gain_rows = keep.tile([P, 2 * P], BF16)
+        gain_col = keep.tile([P, PACK], F32)
+
+        scaled = {}
+        flipped = {}
+        normed = {}
+        unit_now = {}
+
+        def load_x(chunk, part):
+            tiles = slice(part * LOAD_TILES, (part + 1) * LOAD_TILES)
+            first = chunk * CHUNK_TILES + part * LOAD_TILES
+            nc.sync.dma_start(out=x_sb[:, first : first + LOAD_TILES, :], in_=x_chunks[chunk, :, tiles, :])
+
+        def load_weight(which):
+            nc.sync.dma_start(
+                out=w_sb[:, which, :, :], in_=weights[which].rearrange("(fo p) k -> p fo k", p=P)
+            )
+
+        def prepare_weight(which):
+            w_grouped = w_grouped_pool.tile([P, D, PACK], BF16, align_bytes=64)
+            w_grouped_words = w_grouped[:].rearrange("p f t -> p (f t)").bitcast(F32)
+            for half in range(2):
+                w_flip = acc_pool.tile([P, 2, 2, P], F32, tag="acc")
+                for fo in range(2):
+                    w_words = w_sb[:, which, 2 * half + fo, :].bitcast(F32)
+                    for u in range(2):
+                        nc.tensor.transpose(w_flip[:, fo, u, :], w_words[:, u * P : (u + 1) * P], ident_f32[:])
+                words = slice(half * 2 * P * 2, (half + 1) * 2 * P * 2)
+                dst = w_grouped_words[:, words].rearrange("p (fo f u) -> p fo f u", fo=2, u=2)
+                src = w_flip[:].rearrange("p fo u f -> p fo f u")
+                if half == 0:
+                    nc.vector.tensor_copy(out=dst, in_=src)
+                else:
+                    nc.scalar.copy(out=dst, in_=src)
+            nc.vector.quantize_mx(
+                out=w_codes[:, which, :].bitcast(FP8X4),
+                scales=w_scales[:, which, :],
+                in_=w_grouped[:].rearrange("p f t -> p (f t)"),
+            )
+
+        def sum_squares(pair):
+            for i in range(PAIR * pair, PAIR * (pair + 1)):
+                squares = junk_pool.tile([P, D], BF16)
+                nc.scalar.activation(
+                    out=squares[:], in_=x_sb[:, i, :], func=FUNC.Square, accum_out=sum_sq[:, i : i + 1]
+                )
+            cols = slice(PAIR * pair, PAIR * (pair + 1))
+            nc.scalar.activation(
+                out=rms[:, cols], in_=sum_sq[:, cols], func=FUNC.Sqrt, bias=eps_col[:], scale=1.0 / D
+            )
+
+        def scale_rows(pair):
+            cols = slice(PAIR * pair, PAIR * (pair + 1))
+            nc.vector.reciprocal(out=inv_rms[:, cols], in_=rms[:, cols])
+            x_over_rms = scaled_pool.tile([P, PAIR, PACK, P], F32)
+            for h in range(PAIR):
+                i = PAIR * pair + h
+                nc.gpsimd.tensor_scalar(
+                    out=x_over_rms[:, h, :, :].rearrange("l (u e) q -> l u e q", u=2),
+                    in0=x_sb[:, i, :].rearrange("l (u q e) -> l u e q", u=2, e=2),
+                    scalar1=inv_rms[:, i : i + 1],
+                    scalar2=1.0,
+                    op0=MULT,
+                    op1=MULT,
+                )
+            scaled[pair] = x_over_rms
+
+        def transpose_pair(pair):
+            banks = []
+            for h in range(PAIR):
+                x_flip = flip_pool.tile([P, PACK, P], F32, tag="flip")
+                for t in range(PACK):
+                    nc.tensor.transpose(x_flip[:, t, :], scaled[pair][:, h, t, :], ident_f32[:])
+                banks.append(x_flip)
+            flipped[pair] = banks
+
+        def apply_gain(pair):
+            xn = normed_pool.tile([P, PAIR, P, PACK], BF16, align_bytes=64)
+            for h in range(PAIR):
+                nc.vector.tensor_tensor(
+                    out=xn[:, h, :, :],
+                    in0=flipped[pair][h][:].rearrange("p t l -> p l t"),
+                    in1=gain_col[:].unsqueeze(1).to_broadcast([P, P, PACK]),
+                    op=MULT,
+                )
+            normed[pair] = xn
+
+        def quantise(pair):
+            cols = slice(pair * PAIR * P, (pair + 1) * PAIR * P)
+            nc.vector.quantize_mx(
+                out=x_codes[:, cols].bitcast(FP8X4),
+                scales=x_scales[:, cols],
+                in_=normed[pair][:].rearrange("p h l t -> p (h l t)"),
+            )
+
+        def project(bank):
+            chunk, rest = divmod(bank, PROJECTIONS * CHUNK_TILES)
+            which, g = divmod(rest, CHUNK_TILES)
+            if g == 0:
+                unit = unit_pool.tile([P, HEADS, CHUNK_TILES, HEAD_DIM], F32)
+                unit_now["tile"] = unit
+            unit = unit_now["tile"]
+            cols = slice((chunk * CHUNK_TILES + g) * P, (chunk * CHUNK_TILES + g + 1) * P)
+            acc = acc_pool.tile([P, D], F32, tag="acc")
+            nc.tensor.matmul_mx(
+                out=acc[:],
+                lhsT=x_codes[:, cols].bitcast(FP8X4),
+                lhsT_scale=x_scales[:, cols],
+                rhs=w_codes[:, which, :].bitcast(FP8X4),
+                rhs_scale=w_scales[:, which, :],
+                start=True,
+                stop=True,
+            )
+            by_head = acc[:].rearrange("p (n j) -> p n j", n=HEADS)
+            if bank % 2 == 0:
+                nc.scalar.copy(out=unit[:, :, g, :], in_=by_head)
+            else:
+                nc.vector.tensor_copy(out=unit[:, :, g, :], in_=by_head)
+            if g == CHUNK_TILES - 1:
+                batch, part = divmod(chunk, CHUNKS_PER_BATCH)
+                rows = slice(part * CHUNK_TOKENS, (part + 1) * CHUNK_TOKENS)
+                nc.sync.dma_start(
+                    out=outs[which][batch, :, rows, :].rearrange("n (p g) j -> p n (g j)", g=CHUNK_TILES),
+                    in_=unit[:].rearrange("p n g j -> p n (g j)"),
+                )
+
+        nc.vector.memset(eps_col[:], EPS)
+        nc.vector.memset(gain_rows[:], 0.0)
+        make_identity(nc, ident_f32[:])
+        nc.scalar.dma_start(out=gain_rows[0:2, :], in_=attn_norm_w.rearrange("(u c) -> u c", u=2))
+        nc.scalar.activation(out=table_warm[:], in_=eps_col[:], func=FUNC.Sqrt)
+        load_x(0, 0)
+        load_weight(0)
+        load_x(0, 1)
+        load_weight(1)
+        load_weight(2)
+        for chunk in range(1, CHUNKS):
+            for part in range(CHUNK_TILES // LOAD_TILES):
+                load_x(chunk, part)
+
+        for pair in range(STATS_LEAD - QUANT_LEAD):
+            sum_squares(pair)
+            scale_rows(pair)
+        prepare_weight(0)
+        gain_flip = flip_pool.tile([P, P], F32, tag="flip")
+        nc.tensor.transpose(gain_flip[:], gain_rows[:].bitcast(F32), ident_f32[:])
+        nc.vector.tensor_copy(out=gain_col[:], in_=gain_flip[:, 0:2].bitcast(BF16))
+        for pair in range(QUANT_LEAD):
+            transpose_pair(pair)
+            apply_gain(pair)
+            sum_squares(pair + STATS_LEAD - QUANT_LEAD)
+            scale_rows(pair + STATS_LEAD - QUANT_LEAD)
+            quantise(pair)
+
+        for step in range(STEPS):
+            to_quantise = step + QUANT_LEAD
+            to_scale = step + STATS_LEAD
+            first_bank = step * STEP_BANKS
+            if to_quantise < PAIRS:
+                transpose_pair(to_quantise)
+            project(first_bank)
+            project(first_bank + 1)
+            if 1 <= step < PROJECTIONS:
+                prepare_weight(step)
+            if to_quantise < PAIRS:
+                apply_gain(to_quantise)
+            if to_scale < PAIRS:
+                sum_squares(to_scale)
+            project(first_bank + 2)
+            project(first_bank + 3)
+            if to_quantise < PAIRS:
+                quantise(to_quantise)
+            if to_scale < PAIRS:
+                scale_rows(to_scale)
+            project(first_bank + 4)
+            project(first_bank + 5)

@@ -192,6 +192,8 @@ def tile_block_pa_t_kernel(tc, x, attn_norm_w, W_q, W_k, W_v, out_0, out_1, out_
                     in_=unit[:].rearrange("p n g j -> p n (g j)"),
                 )
 
+        stack.enter_context(tc.manual_schedule())
+
         nc.vector.memset(eps_col[:], EPS)
         nc.vector.memset(gain_rows[:], 0.0)
         make_identity(nc, ident_f32[:])

@@ -26,14 +26,13 @@ CHUNK_TOKENS = P * CHUNK_TILES
 CHUNKS_PER_BATCH = SEQ // CHUNK_TOKENS
 CHUNKS = BATCH * CHUNKS_PER_BATCH
 TOKEN_TILES = CHUNKS * CHUNK_TILES
-LOAD_TILES = 4
 
 PAIR = 2
 PAIRS = TOKEN_TILES // PAIR
+CHUNK_PAIRS = CHUNK_TILES // PAIR
 STEP_BANKS = PAIR * PROJECTIONS
-STEPS = PAIRS
-QUANT_LEAD = 3
-STATS_LEAD = 5
+QUANT_LEAD = 4
+STATS_LEAD = 6
 
 FLOPS = 2 * BATCH * SEQ * D * PROJECTIONS * D
 
@@ -74,10 +73,12 @@ def tile_block_pa_t_kernel(tc, x, attn_norm_w, W_q, W_k, W_v, out_0, out_1, out_
         normed = {}
         unit_now = {}
 
-        def load_x(chunk, part):
-            tiles = slice(part * LOAD_TILES, (part + 1) * LOAD_TILES)
-            first = chunk * CHUNK_TILES + part * LOAD_TILES
-            nc.sync.dma_start(out=x_sb[:, first : first + LOAD_TILES, :], in_=x_chunks[chunk, :, tiles, :])
+        def load_x(pair):
+            chunk, part = divmod(pair, CHUNK_PAIRS)
+            nc.sync.dma_start(
+                out=x_sb[:, PAIR * pair : PAIR * (pair + 1), :],
+                in_=x_chunks[chunk, :, PAIR * part : PAIR * (part + 1), :],
+            )
 
         def load_weight(which):
             nc.sync.dma_start(
@@ -184,12 +185,16 @@ def tile_block_pa_t_kernel(tc, x, attn_norm_w, W_q, W_k, W_v, out_0, out_1, out_
                 nc.scalar.copy(out=unit[:, :, g, :], in_=by_head)
             else:
                 nc.vector.tensor_copy(out=unit[:, :, g, :], in_=by_head)
-            if g == CHUNK_TILES - 1:
+            store_tiles = CHUNK_TILES // 2 if chunk == 0 else CHUNK_TILES
+            if (g + 1) % store_tiles == 0:
                 batch, part = divmod(chunk, CHUNKS_PER_BATCH)
                 rows = slice(part * CHUNK_TOKENS, (part + 1) * CHUNK_TOKENS)
+                tiles = slice(g + 1 - store_tiles, g + 1)
                 nc.sync.dma_start(
-                    out=outs[which][batch, :, rows, :].rearrange("n (p g) j -> p n (g j)", g=CHUNK_TILES),
-                    in_=unit[:].rearrange("p n g j -> p n (g j)"),
+                    out=outs[which][batch, :, rows, :].rearrange("n (p g) j -> p n g j", g=CHUNK_TILES)[
+                        :, :, tiles, :
+                    ],
+                    in_=unit[:, :, tiles, :],
                 )
 
         stack.enter_context(tc.manual_schedule())
@@ -199,20 +204,21 @@ def tile_block_pa_t_kernel(tc, x, attn_norm_w, W_q, W_k, W_v, out_0, out_1, out_
         make_identity(nc, ident_f32[:])
         nc.scalar.dma_start(out=gain_rows[0:2, :], in_=attn_norm_w.rearrange("(u c) -> u c", u=2))
         nc.scalar.activation(out=table_warm[:], in_=eps_col[:], func=FUNC.Sqrt)
-        load_x(0, 0)
+        load_x(0)
+        load_x(1)
         load_weight(0)
-        load_x(0, 1)
+        load_x(2)
+        load_x(3)
         load_weight(1)
         load_weight(2)
-        for chunk in range(1, CHUNKS):
-            for part in range(CHUNK_TILES // LOAD_TILES):
-                load_x(chunk, part)
+        for pair in range(CHUNK_PAIRS, PAIRS):
+            load_x(pair)
 
         for pair in range(STATS_LEAD - QUANT_LEAD):
             sum_squares(pair)
             scale_rows(pair)
         prepare_weight(0)
-        gain_flip = flip_pool.tile([P, P], F32, tag="flip")
+        gain_flip = acc_pool.tile([P, P], F32, tag="acc")
         nc.tensor.transpose(gain_flip[:], gain_rows[:].bitcast(F32), ident_f32[:])
         nc.vector.tensor_copy(out=gain_col[:], in_=gain_flip[:, 0:2].bitcast(BF16))
         for pair in range(QUANT_LEAD):
@@ -221,17 +227,19 @@ def tile_block_pa_t_kernel(tc, x, attn_norm_w, W_q, W_k, W_v, out_0, out_1, out_
             sum_squares(pair + STATS_LEAD - QUANT_LEAD)
             scale_rows(pair + STATS_LEAD - QUANT_LEAD)
             quantise(pair)
+            if pair >= 1:
+                project(PAIR * (pair - 1))
+                project(PAIR * (pair - 1) + 1)
+        prepare_weight(1)
+        prepare_weight(2)
 
-        for step in range(STEPS):
-            to_quantise = step + QUANT_LEAD
-            to_scale = step + STATS_LEAD
-            first_bank = step * STEP_BANKS
+        for first_bank in range(STEP_BANKS, PROJECTIONS * TOKEN_TILES, STEP_BANKS):
+            to_quantise = first_bank // STEP_BANKS - 1 + QUANT_LEAD
+            to_scale = first_bank // STEP_BANKS - 1 + STATS_LEAD
             if to_quantise < PAIRS:
                 transpose_pair(to_quantise)
             project(first_bank)
             project(first_bank + 1)
-            if 1 <= step < PROJECTIONS:
-                prepare_weight(step)
             if to_quantise < PAIRS:
                 apply_gain(to_quantise)
             if to_scale < PAIRS:

@@ -60,7 +60,6 @@ def tile_block_pa_t_kernel(tc, x, attn_norm_w, W_q, W_k, W_v, out_0, out_1, out_
         x_codes = keep.tile([P, TOKEN_TILES * P], U32, align_bytes=64)
         x_scales = keep.tile([P, TOKEN_TILES * P], U8, align_bytes=64)
         sum_sq = keep.tile([P, TOKEN_TILES], F32)
-        rms = keep.tile([P, TOKEN_TILES], F32)
         inv_rms = keep.tile([P, TOKEN_TILES], F32)
         ident_f32 = keep.tile([P, P], F32)
         eps_col = keep.tile([P, 1], F32)
@@ -115,12 +114,14 @@ def tile_block_pa_t_kernel(tc, x, attn_norm_w, W_q, W_k, W_v, out_0, out_1, out_
                 )
             cols = slice(PAIR * pair, PAIR * (pair + 1))
             nc.scalar.activation(
-                out=rms[:, cols], in_=sum_sq[:, cols], func=FUNC.Sqrt, bias=eps_col[:], scale=1.0 / D
+                out=inv_rms[:, cols],
+                in_=sum_sq[:, cols],
+                func=FUNC.Abs_reciprocal_sqrt,
+                bias=eps_col[:],
+                scale=1.0 / D,
             )
 
         def scale_rows(pair):
-            cols = slice(PAIR * pair, PAIR * (pair + 1))
-            nc.vector.reciprocal(out=inv_rms[:, cols], in_=rms[:, cols])
             x_over_rms = scaled_pool.tile([P, PAIR, PACK, P], F32)
             for h in range(PAIR):
                 i = PAIR * pair + h
@@ -203,7 +204,7 @@ def tile_block_pa_t_kernel(tc, x, attn_norm_w, W_q, W_k, W_v, out_0, out_1, out_
         nc.vector.memset(gain_rows[:], 0.0)
         make_identity(nc, ident_f32[:])
         nc.scalar.dma_start(out=gain_rows[0:2, :], in_=attn_norm_w.rearrange("(u c) -> u c", u=2))
-        nc.scalar.activation(out=table_warm[:], in_=eps_col[:], func=FUNC.Sqrt)
+        nc.scalar.activation(out=table_warm[:], in_=eps_col[:], func=FUNC.Abs_reciprocal_sqrt)
         load_x(0)
         load_x(1)
         load_weight(0)

@@ -22,6 +22,7 @@ EPS = 1e-6
 PROJECTIONS = 3
 
 CHUNK_TILES = 8
+STORE_HEADS = 4
 CHUNK_TOKENS = P * CHUNK_TILES
 CHUNKS_PER_BATCH = SEQ // CHUNK_TOKENS
 CHUNKS = BATCH * CHUNKS_PER_BATCH
@@ -60,6 +61,7 @@ def tile_block_pa_t_kernel(tc, x, attn_norm_w, W_q, W_k, W_v, out_0, out_1, out_
         x_codes = keep.tile([P, TOKEN_TILES * P], U32, align_bytes=64)
         x_scales = keep.tile([P, TOKEN_TILES * P], U8, align_bytes=64)
         sum_sq = keep.tile([P, TOKEN_TILES], F32)
+        rms = keep.tile([P, TOKEN_TILES], F32)
         inv_rms = keep.tile([P, TOKEN_TILES], F32)
         ident_f32 = keep.tile([P, P], F32)
         eps_col = keep.tile([P, 1], F32)
@@ -114,14 +116,12 @@ def tile_block_pa_t_kernel(tc, x, attn_norm_w, W_q, W_k, W_v, out_0, out_1, out_
                 )
             cols = slice(PAIR * pair, PAIR * (pair + 1))
             nc.scalar.activation(
-                out=inv_rms[:, cols],
-                in_=sum_sq[:, cols],
-                func=FUNC.Abs_reciprocal_sqrt,
-                bias=eps_col[:],
-                scale=1.0 / D,
+                out=rms[:, cols], in_=sum_sq[:, cols], func=FUNC.Sqrt, bias=eps_col[:], scale=1.0 / D
             )
 
         def scale_rows(pair):
+            cols = slice(PAIR * pair, PAIR * (pair + 1))
+            nc.vector.reciprocal(out=inv_rms[:, cols], in_=rms[:, cols])
             x_over_rms = scaled_pool.tile([P, PAIR, PACK, P], F32)
             for h in range(PAIR):
                 i = PAIR * pair + h
@@ -191,12 +191,10 @@ def tile_block_pa_t_kernel(tc, x, attn_norm_w, W_q, W_k, W_v, out_0, out_1, out_
                 batch, part = divmod(chunk, CHUNKS_PER_BATCH)
                 rows = slice(part * CHUNK_TOKENS, (part + 1) * CHUNK_TOKENS)
                 tiles = slice(g + 1 - store_tiles, g + 1)
-                nc.sync.dma_start(
-                    out=outs[which][batch, :, rows, :].rearrange("n (p g) j -> p n g j", g=CHUNK_TILES)[
-                        :, :, tiles, :
-                    ],
-                    in_=unit[:, :, tiles, :],
-                )
+                out_view = outs[which][batch, :, rows, :].rearrange("n (p g) j -> p n g j", g=CHUNK_TILES)
+                for first_head in range(0, HEADS, STORE_HEADS):
+                    heads = slice(first_head, first_head + STORE_HEADS)
+                    nc.sync.dma_start(out=out_view[:, heads, tiles, :], in_=unit[:, heads, tiles, :])
 
         stack.enter_context(tc.manual_schedule())
 
@@ -204,7 +202,7 @@ def tile_block_pa_t_kernel(tc, x, attn_norm_w, W_q, W_k, W_v, out_0, out_1, out_
         nc.vector.memset(gain_rows[:], 0.0)
         make_identity(nc, ident_f32[:])
         nc.scalar.dma_start(out=gain_rows[0:2, :], in_=attn_norm_w.rearrange("(u c) -> u c", u=2))
-        nc.scalar.activation(out=table_warm[:], in_=eps_col[:], func=FUNC.Abs_reciprocal_sqrt)
+        nc.scalar.activation(out=table_warm[:], in_=eps_col[:], func=FUNC.Sqrt)
         load_x(0)
         load_x(1)
         load_weight(0)

from contextlib import ExitStack

import concourse.mybir as mybir
from concourse.masks import make_identity

BF16 = mybir.dt.bfloat16
F32 = mybir.dt.float32
U32 = mybir.dt.uint32
U8 = mybir.dt.uint8
FP8X4 = mybir.dt.float8_e4m3fn_x4
MULT = mybir.AluOpType.mult
FUNC = mybir.ActivationFunctionType

P = 128
PACK = 4
D = P * PACK
BATCH = 2
SEQ = 2048
HEADS = 8
HEAD_DIM = D // HEADS
EPS = 1e-6
PROJECTIONS = 3

CHUNK_TILES = 8
STORE_HEADS = 4
CHUNK_TOKENS = P * CHUNK_TILES
CHUNKS_PER_BATCH = SEQ // CHUNK_TOKENS
CHUNKS = BATCH * CHUNKS_PER_BATCH
TOKEN_TILES = CHUNKS * CHUNK_TILES

PAIR = 2
PAIRS = TOKEN_TILES // PAIR
CHUNK_PAIRS = CHUNK_TILES // PAIR
STEP_BANKS = PAIR * PROJECTIONS
QUANT_LEAD = 4
STATS_LEAD = 6

FLOPS = 2 * BATCH * SEQ * D * PROJECTIONS * D


def tile_block_pa_t_kernel(tc, x, attn_norm_w, W_q, W_k, W_v, out_0, out_1, out_2):
    nc = tc.nc
    weights = (W_q, W_k, W_v)
    outs = (out_0, out_1, out_2)
    x_chunks = x.flatten_outer_dims().rearrange("(c p g) d -> c p g d", p=P, g=CHUNK_TILES)

    with ExitStack() as stack:
        keep = stack.enter_context(tc.tile_pool(name="keep", bufs=1))
        junk_pool = stack.enter_context(tc.tile_pool(name="junk", bufs=2))
        scaled_pool = stack.enter_context(tc.tile_pool(name="scaled", bufs=3))
        normed_pool = stack.enter_context(tc.tile_pool(name="normed", bufs=2))
        w_grouped_pool = stack.enter_context(tc.tile_pool(name="w_grouped", bufs=2))
        unit_pool = stack.enter_context(tc.tile_pool(name="unit", bufs=6))
        flip_pool = stack.enter_context(tc.psum_pool(name="flip", bufs=2))
        acc_pool = stack.enter_context(tc.psum_pool(name="acc", bufs=STEP_BANKS))

        x_sb = keep.tile([P, TOKEN_TILES, D], BF16)
        w_sb = keep.tile([P, PROJECTIONS, PACK, D], BF16)
        w_codes = keep.tile([P, PROJECTIONS, D], U32, align_bytes=64)
        w_scales = keep.tile([P, PROJECTIONS, D], U8, align_bytes=64)
        x_codes = keep.tile([P, TOKEN_TILES * P], U32, align_bytes=64)
        x_scales = keep.tile([P, TOKEN_TILES * P], U8, align_bytes=64)
        sum_sq = keep.tile([P, TOKEN_TILES], F32)
        rms = keep.tile([P, TOKEN_TILES], F32)
        inv_rms = keep.tile([P, TOKEN_TILES], F32)
        ident_f32 = keep.tile([P, P], F32)
        eps_col = keep.tile([P, 1], F32)
        table_warm = keep.tile([P, 1], F32)
        gain_rows = keep.tile([P, 2 * P], BF16)
        gain_col = keep.tile([P, PACK], F32)

        scaled = {}
        flipped = {}
        normed = {}
        unit_now = {}

        def load_x(pair):
            chunk, part = divmod(pair, CHUNK_PAIRS)
            nc.sync.dma_start(
                out=x_sb[:, PAIR * pair : PAIR * (pair + 1), :],
                in_=x_chunks[chunk, :, PAIR * part : PAIR * (part + 1), :],
            )

        def load_weight(which):
            nc.sync.dma_start(
                out=w_sb[:, which, :, :], in_=weights[which].rearrange("(fo p) k -> p fo k", p=P)
            )

        def prepare_weight(which):
            w_grouped = w_grouped_pool.tile([P, D, PACK], BF16, align_bytes=64)
            w_grouped_words = w_grouped[:].rearrange("p f t -> p (f t)").bitcast(F32)
            for half in range(2):
                w_flip = acc_pool.tile([P, 2, 2, P], F32, tag="acc")
                for fo in range(2):
                    w_words = w_sb[:, which, 2 * half + fo, :].bitcast(F32)
                    for u in range(2):
                        nc.tensor.transpose(w_flip[:, fo, u, :], w_words[:, u * P : (u + 1) * P], ident_f32[:])
                words = slice(half * 2 * P * 2, (half + 1) * 2 * P * 2)
                dst = w_grouped_words[:, words].rearrange("p (fo f u) -> p fo f u", fo=2, u=2)
                src = w_flip[:].rearrange("p fo u f -> p fo f u")
                if half == 0:
                    nc.vector.tensor_copy(out=dst, in_=src)
                else:
                    nc.scalar.copy(out=dst, in_=src)
            nc.vector.quantize_mx(
                out=w_codes[:, which, :].bitcast(FP8X4),
                scales=w_scales[:, which, :],
                in_=w_grouped[:].rearrange("p f t -> p (f t)"),
            )

        def sum_squares(pair):
            for i in range(PAIR * pair, PAIR * (pair + 1)):
                squares = junk_pool.tile([P, D], BF16)
                nc.scalar.activation(
                    out=squares[:], in_=x_sb[:, i, :], func=FUNC.Square, accum_out=sum_sq[:, i : i + 1]
                )
            cols = slice(PAIR * pair, PAIR * (pair + 1))
            nc.scalar.activation(
                out=rms[:, cols], in_=sum_sq[:, cols], func=FUNC.Sqrt, bias=eps_col[:], scale=1.0 / D
            )

        def scale_rows(pair):
            cols = slice(PAIR * pair, PAIR * (pair + 1))
            nc.vector.reciprocal(out=inv_rms[:, cols], in_=rms[:, cols])
            x_over_rms = scaled_pool.tile([P, PAIR, PACK, P], F32)
            for h in range(PAIR):
                i = PAIR * pair + h
                nc.gpsimd.tensor_scalar(
                    out=x_over_rms[:, h, :, :].rearrange("l (u e) q -> l u e q", u=2),
                    in0=x_sb[:, i, :].rearrange("l (u q e) -> l u e q", u=2, e=2),
                    scalar1=inv_rms[:, i : i + 1],
                    scalar2=1.0,
                    op0=MULT,
                    op1=MULT,
                )
            scaled[pair] = x_over_rms

        def transpose_pair(pair):
            banks = []
            for h in range(PAIR):
                x_flip = flip_pool.tile([P, PACK, P], F32, tag="flip")
                for t in range(PACK):
                    nc.tensor.transpose(x_flip[:, t, :], scaled[pair][:, h, t, :], ident_f32[:])
                banks.append(x_flip)
            flipped[pair] = banks

        def apply_gain(pair):
            xn = normed_pool.tile([P, PAIR, P, PACK], BF16, align_bytes=64)
            for h in range(PAIR):
                nc.vector.tensor_tensor(
                    out=xn[:, h, :, :],
                    in0=flipped[pair][h][:].rearrange("p t l -> p l t"),
                    in1=gain_col[:].unsqueeze(1).to_broadcast([P, P, PACK]),
                    op=MULT,
                )
            normed[pair] = xn

        def quantise(pair):
            cols = slice(pair * PAIR * P, (pair + 1) * PAIR * P)
            nc.vector.quantize_mx(
                out=x_codes[:, cols].bitcast(FP8X4),
                scales=x_scales[:, cols],
                in_=normed[pair][:].rearrange("p h l t -> p (h l t)"),
            )

        def project(bank):
            chunk, rest = divmod(bank, PROJECTIONS * CHUNK_TILES)
            which, g = divmod(rest, CHUNK_TILES)
            if g == 0:
                unit = unit_pool.tile([P, HEADS, CHUNK_TILES, HEAD_DIM], F32)
                unit_now["tile"] = unit
            unit = unit_now["tile"]
            cols = slice((chunk * CHUNK_TILES + g) * P, (chunk * CHUNK_TILES + g + 1) * P)
            acc = acc_pool.tile([P, D], F32, tag="acc")
            nc.tensor.matmul_mx(
                out=acc[:],
                lhsT=x_codes[:, cols].bitcast(FP8X4),
                lhsT_scale=x_scales[:, cols],
                rhs=w_codes[:, which, :].bitcast(FP8X4),
                rhs_scale=w_scales[:, which, :],
                start=True,
                stop=True,
            )
            by_head = acc[:].rearrange("p (n j) -> p n j", n=HEADS)
            if bank % 2 == 0:
                nc.scalar.copy(out=unit[:, :, g, :], in_=by_head)
            else:
                nc.vector.tensor_copy(out=unit[:, :, g, :], in_=by_head)
            store_tiles = CHUNK_TILES // 2 if chunk == 0 else CHUNK_TILES
            if (g + 1) % store_tiles == 0:
                batch, part = divmod(chunk, CHUNKS_PER_BATCH)
                rows = slice(part * CHUNK_TOKENS, (part + 1) * CHUNK_TOKENS)
                tiles = slice(g + 1 - store_tiles, g + 1)
                out_view = outs[which][batch, :, rows, :].rearrange("n (p g) j -> p n g j", g=CHUNK_TILES)
                for first_head in range(0, HEADS, STORE_HEADS):
                    heads = slice(first_head, first_head + STORE_HEADS)
                    nc.sync.dma_start(out=out_view[:, heads, tiles, :], in_=unit[:, heads, tiles, :])

        stack.enter_context(tc.manual_schedule())

        nc.vector.memset(eps_col[:], EPS)
        nc.vector.memset(gain_rows[:], 0.0)
        make_identity(nc, ident_f32[:])
        nc.scalar.dma_start(out=gain_rows[0:2, :], in_=attn_norm_w.rearrange("(u c) -> u c", u=2))
        nc.scalar.activation(out=table_warm[:], in_=eps_col[:], func=FUNC.Sqrt)
        load_x(0)
        load_x(1)
        load_weight(0)
        load_x(2)
        load_x(3)
        load_weight(1)
        load_weight(2)
        for pair in range(CHUNK_PAIRS, PAIRS):
            load_x(pair)

        for pair in range(STATS_LEAD - QUANT_LEAD):
            sum_squares(pair)
            scale_rows(pair)
        prepare_weight(0)
        gain_flip = acc_pool.tile([P, P], F32, tag="acc")
        nc.tensor.transpose(gain_flip[:], gain_rows[:].bitcast(F32), ident_f32[:])
        nc.vector.tensor_copy(out=gain_col[:], in_=gain_flip[:, 0:2].bitcast(BF16))
        for pair in range(QUANT_LEAD):
            transpose_pair(pair)
            apply_gain(pair)
            sum_squares(pair + STATS_LEAD - QUANT_LEAD)
            scale_rows(pair + STATS_LEAD - QUANT_LEAD)
            quantise(pair)
            if pair >= 1:
                project(PAIR * (pair - 1))
                project(PAIR * (pair - 1) + 1)
        prepare_weight(1)
        prepare_weight(2)

        for first_bank in range(STEP_BANKS, PROJECTIONS * TOKEN_TILES, STEP_BANKS):
            to_quantise = first_bank // STEP_BANKS - 1 + QUANT_LEAD
            to_scale = first_bank // STEP_BANKS - 1 + STATS_LEAD
            if to_quantise < PAIRS:
                transpose_pair(to_quantise)
            project(first_bank)
            project(first_bank + 1)
            if to_quantise < PAIRS:
                apply_gain(to_quantise)
            if to_scale < PAIRS:
                sum_squares(to_scale)
            project(first_bank + 2)
            project(first_bank + 3)
            if to_quantise < PAIRS:
                quantise(to_quantise)
            if to_scale < PAIRS:
                scale_rows(to_scale)
            project(first_bank + 4)
            project(first_bank + 5)
